import numpy as np
import ml_dtypes


def mxq(x, axis, fmt="e4m3"):
    dtype, down = {"e4m3": (ml_dtypes.float8_e4m3fn, 7), "e5m2": (ml_dtypes.float8_e5m2, 14)}[fmt]
    v = np.moveaxis(np.asarray(x, np.float32).astype(ml_dtypes.bfloat16).astype(np.float64), axis, -1)
    blocks = v.reshape(v.shape[:-1] + (-1, 32))
    amax = np.abs(blocks).max(-1, keepdims=True)
    byte = np.maximum(np.where(amax > 0, np.frexp(amax)[1] - 1 + 127, 0) - down, 1)
    scale = np.exp2(byte - 127.0)
    codes = (blocks / scale).astype(np.float32).astype(dtype).astype(np.float64)
    return np.moveaxis((codes * scale).reshape(v.shape), -1, axis)


WIDE = False


def mx_kscale(k):
    if not WIDE:
        return np.ones(k)
    levels = np.array([10, -10, 5, -5, 0])
    a = np.random.permutation(np.resize(levels, k // 512 * 4)).reshape(k // 512, 4)
    idx = np.arange(k)
    return np.exp2(a[idx // 512, idx % 128 // 32])


BF16 = ml_dtypes.bfloat16


def bf(x):
    return np.asarray(x, np.float32).astype(BF16)


def f64(x):
    return np.asarray(x).astype(np.float64)


E2M1 = np.array([0.0, 0.5, 1.0, 1.5, 2.0, 3.0, 4.0, 6.0, -0.0, -0.5, -1.0, -1.5, -2.0, -3.0, -4.0, -6.0])


def pack_weight(w, fmt):
    k, n = w.shape
    w = f64(bf(w)).reshape(k // 32, 32, n)
    amax = np.abs(w).max(1)
    if fmt == "e4m3":
        byte = np.frexp(amax)[1] - 1 + 127 - 7
    else:
        mant, ex = np.frexp(amax / 6.0)
        byte = np.where(mant > 0.5, ex, ex - 1) + 127
    byte = np.clip(np.where(amax > 0, byte, 1), 1, 254)
    scaled = (w * np.exp2(127.0 - byte)[:, None, :]).reshape(k, n).astype(np.float32)
    by_word = np.ascontiguousarray(scaled.reshape(k // 512, 128, 4, n).transpose(0, 1, 3, 2))
    if fmt == "e4m3":
        words = by_word.astype(ml_dtypes.float8_e4m3fn).view(np.uint8)
    else:
        c = by_word.astype(ml_dtypes.float4_e2m1fn).view(np.uint8) & 0xF
        words = c[..., 0::2] | (c[..., 1::2] << 4)
    return np.ascontiguousarray(words), np.ascontiguousarray(byte.astype(np.uint8).reshape(k // 512, 16, n))


def unpack_weight(words, scales, fmt):
    g, p, n, _ = words.shape
    if fmt == "e4m3":
        vals = np.ascontiguousarray(words).view(ml_dtypes.float8_e4m3fn).astype(np.float64)
    else:
        nib = np.empty((g, p, n, 4), np.uint8)
        nib[..., 0::2] = words & 0xF
        nib[..., 1::2] = words >> 4
        vals = E2M1[nib]
    vals = vals * np.repeat(np.exp2(scales.astype(np.float64) - 127.0), 8, axis=1)[..., None]
    return vals.transpose(0, 1, 3, 2).reshape(g * 512, n)


B, S, D_IN, MID, FFN, D_OUT, R = 2, 128, 256, 1024, 16384, 512, 16
LN_EPS = 1e-5
FMT = "e4m3"


def silu(v):
    return v / (1.0 + np.exp(-v))


def layer_norm(x, gamma, beta):
    m = np.mean(x, axis=-1, keepdims=True)
    v = np.mean(np.square(x - m), axis=-1, keepdims=True)
    return (x - m) / np.sqrt(v + LN_EPS) * gamma + beta


def setup_inputs():
    t, s = mx_kscale(FFN), mx_kscale(MID)
    h = bf(silu(np.random.standard_normal((B, S, FFN))) * t)
    w_f2 = np.random.standard_normal((MID, FFN)) / np.sqrt(FFN) / t
    b_f2 = bf(0.1 * np.random.standard_normal(MID))
    res1 = bf(0.7 * np.random.standard_normal((B, S, MID)))
    g2 = bf((1.0 + 0.1 * np.random.standard_normal(MID)) * s)
    be2 = bf(0.1 * np.random.standard_normal(MID) * s)
    w_h = np.random.standard_normal((D_OUT, MID)) / np.sqrt(MID) / s
    b_h = bf(0.1 * np.random.standard_normal(D_OUT))
    w_f2_words, w_f2_scales = pack_weight(np.ascontiguousarray(w_f2.T), FMT)
    w_h_words, w_h_scales = pack_weight(np.ascontiguousarray(w_h.T), FMT)
    return {"h": h,
            "w_f2_words": w_f2_words,
            "w_f2_scales": w_f2_scales,
            "b_f2": b_f2,
            "res1": res1,
            "g2": g2,
            "be2": be2,
            "w_h_words": w_h_words,
            "w_h_scales": w_h_scales,
            "b_h": b_h}


def reference(h, w_f2_words, w_f2_scales, b_f2, res1, g2, be2, w_h_words, w_h_scales, b_h):
    ffn = (mxq(f64(h), 2, "e4m3") @ unpack_weight(w_f2_words, w_f2_scales, FMT)) + f64(b_f2)
    res2 = f64(res1) + ffn
    norm2 = layer_norm(res2, f64(g2), f64(be2))
    return (mxq(norm2, 2, "e4m3") @ unpack_weight(w_h_words, w_h_scales, FMT)) + f64(b_h)

@@ -1,0 +1,297 @@
+from contextlib import ExitStack
+
+import concourse.mybir as mybir
+from concourse.masks import make_identity
+
+F32 = mybir.dt.float32
+BF16 = mybir.dt.bfloat16
+I32 = mybir.dt.int32
+U32 = mybir.dt.uint32
+U8 = mybir.dt.uint8
+FP8X4 = mybir.dt.float8_e4m3fn_x4
+ALU = mybir.AluOpType
+ACT = mybir.ActivationFunctionType
+
+P = 128
+PACK = 4
+K_PASS = P * PACK
+BANK = 512
+
+TOKEN_TILES = 2
+FFN = 16384
+MID = 1024
+D_OUT = 512
+LN_EPS = 1e-5
+FFN_PASSES = FFN // K_PASS
+MID_PASSES = MID // K_PASS
+
+H_CHUNK_PASSES = 8
+QUANT_PASSES = 4
+BANK_PASSES = 2
+W_CHUNK_PASSES = 2
+W_BUFS = 7
+PLANES_PER_TILE = 4
+
+FLOPS = 2 * TOKEN_TILES * P * (FFN * MID + MID * D_OUT)
+
+
+def word_order(columns):
+    return columns.rearrange("p (j t) -> p t j", t=PACK)
+
+
+def as_t_j(columns):
+    return columns.rearrange("p (t j) -> p t j", t=PACK)
+
+
+def tile_tsh_mid_block_pb_k_kernel(
+    tc, h, w_f2_words, w_f2_scales, b_f2, res1, g2, be2, w_h_words, w_h_scales, b_h, out
+):
+    nc = tc.nc
+    with ExitStack() as stack:
+        keep = stack.enter_context(tc.tile_pool(name="keep", bufs=1))
+        w_stream = stack.enter_context(tc.tile_pool(name="w_stream", bufs=W_BUFS))
+        psum_acc = stack.enter_context(tc.psum_pool(name="psum_acc", bufs=1))
+        psum_work = stack.enter_context(tc.psum_pool(name="psum_work", bufs=4))
+
+        ident_f32 = keep.tile([P, P], F32, name="ident_f32")
+        make_identity(nc, ident_f32[:])
+        ident_bf16 = keep.tile([P, P], BF16, name="ident_bf16")
+        make_identity(nc, ident_bf16[:])
+        ones = keep.tile([P, P], BF16, name="ones")
+        nc.vector.memset(ones[:], 1.0)
+        eps = keep.tile([P, 1], F32, name="eps")
+        nc.vector.memset(eps[:], LN_EPS)
+        table_warm = keep.tile([P, 1], F32, name="table_warm")
+        nc.scalar.activation(out=table_warm[:], in_=eps[:], func=ACT.Sqrt)
+
+        w_planes = keep.tile(
+            [P, FFN_PASSES // PLANES_PER_TILE, MID], U8, name="w_planes", align_bytes=64
+        )
+        nc.vector.memset(w_planes[:].bitcast(I32), 0)
+        wh_planes = keep.tile([P, MID_PASSES, D_OUT], U8, name="wh_planes", align_bytes=64)
+        nc.vector.memset(wh_planes[:].bitcast(I32), 0)
+
+        h_codes = keep.tile([P, TOKEN_TILES, FFN_PASSES, P], U32, name="h_codes", align_bytes=64)
+        h_scales = keep.tile([P, TOKEN_TILES, FFN_PASSES, P], U8, name="h_scales", align_bytes=64)
+        bias_f2_all = keep.tile([P, MID], F32, name="bias_f2_all")
+        gain_all = keep.tile([P, MID], F32, name="gain_all")
+        shift_all = keep.tile([P, MID], F32, name="shift_all")
+        bias_h_all = keep.tile([P, D_OUT], F32, name="bias_h_all")
+
+        with ExitStack() as part1:
+            h_pool = part1.enter_context(
+                tc.tile_pool(name="h_raw", bufs=TOKEN_TILES * FFN_PASSES // H_CHUNK_PASSES)
+            )
+            stage = part1.enter_context(tc.tile_pool(name="stage", bufs=4))
+            rows_pool = part1.enter_context(tc.tile_pool(name="rows", bufs=1))
+
+            vector_rows = rows_pool.tile([P, 3 * MID + D_OUT], BF16, name="vector_rows")
+            nc.vector.memset(vector_rows[:].bitcast(I32), 0)
+            for position, vector in enumerate((b_f2, g2, be2)):
+                nc.scalar.dma_start(
+                    out=vector_rows[0:1, position * MID : (position + 1) * MID],
+                    in_=vector.rearrange("(o n) -> o n", o=1),
+                )
+            nc.scalar.dma_start(
+                out=vector_rows[0:1, 3 * MID :], in_=b_h.rearrange("(o n) -> o n", o=1)
+            )
+
+            banks_emptied = 0
+            for chunk in range(FFN_PASSES // H_CHUNK_PASSES):
+                for i in range(TOKEN_TILES):
+                    h_raw = h_pool.tile([P, H_CHUNK_PASSES * K_PASS], BF16, name="h_raw")
+                    first_k = chunk * H_CHUNK_PASSES * K_PASS
+                    nc.sync.dma_start(
+                        out=h_raw[:], in_=h[i, :, first_k : first_k + H_CHUNK_PASSES * K_PASS]
+                    )
+                    h_pairs = h_raw[:].bitcast(F32)
+                    for quarter in range(H_CHUNK_PASSES // QUANT_PASSES):
+                        grouped = stage.tile(
+                            [P, QUANT_PASSES * P * PACK], BF16, name="grouped", align_bytes=64
+                        )
+                        grouped_pairs = grouped[:].bitcast(F32).rearrange(
+                            "p (g r u) -> p g r u", g=QUANT_PASSES, r=P
+                        )
+                        for bank in range(QUANT_PASSES // BANK_PASSES):
+                            turned = psum_work.tile([P, BANK_PASSES, 2, P], F32, name="turned", tag="work")
+                            for g_in_bank in range(BANK_PASSES):
+                                g_in_chunk = quarter * QUANT_PASSES + bank * BANK_PASSES + g_in_bank
+                                first_pair = g_in_chunk * K_PASS // 2
+                                for u in range(2):
+                                    nc.tensor.transpose(
+                                        turned[:, g_in_bank, u, :],
+                                        h_pairs[:, first_pair + u : first_pair + K_PASS // 2 : 2],
+                                        ident_f32[:],
+                                    )
+                            target = grouped_pairs[:, bank * BANK_PASSES : (bank + 1) * BANK_PASSES]
+                            source = turned[:].rearrange("p g u r -> p g r u")
+                            if banks_emptied % 4 == 3:
+                                nc.vector.tensor_copy(out=target, in_=source)
+                            else:
+                                nc.scalar.copy(out=target, in_=source)
+                            banks_emptied += 1
+                        g0 = chunk * H_CHUNK_PASSES + quarter * QUANT_PASSES
+                        nc.vector.quantize_mx(
+                            out=h_codes[:, i, g0 : g0 + QUANT_PASSES, :]
+                            .rearrange("p g r -> p (g r)")
+                            .bitcast(FP8X4),
+                            scales=h_scales[:, i, g0 : g0 + QUANT_PASSES, :].rearrange("p g r -> p (g r)"),
+                            in_=grouped[:],
+                        )
+
+            spread_targets = (
+                [as_t_j(bias_f2_all[:, g * BANK : (g + 1) * BANK]) for g in range(MID_PASSES)]
+                + [as_t_j(gain_all[:, g * BANK : (g + 1) * BANK]) for g in range(MID_PASSES)]
+                + [as_t_j(shift_all[:, g * BANK : (g + 1) * BANK]) for g in range(MID_PASSES)]
+            )
+            for position, target in enumerate(spread_targets):
+                spread = psum_work.tile([P, BANK], F32, name="spread", tag="work")
+                nc.tensor.matmul(
+                    out=spread[:],
+                    lhsT=ones[:],
+                    rhs=vector_rows[:, position * BANK : (position + 1) * BANK],
+                    start=True,
+                    stop=True,
+                )
+                nc.scalar.copy(out=target, in_=word_order(spread[:]))
+            spread = psum_work.tile([P, BANK], F32, name="spread", tag="work")
+            nc.tensor.matmul(
+                out=spread[:], lhsT=ones[:], rhs=vector_rows[:, 3 * MID :], start=True, stop=True
+            )
+            nc.scalar.copy(out=bias_h_all[:], in_=spread[:])
+
+        residual = []
+        for i in range(TOKEN_TILES):
+            res1_raw = keep.tile([P, MID], BF16, name="res1_raw_%d" % i)
+            nc.sync.dma_start(out=res1_raw[:], in_=res1[i])
+            residual_i = keep.tile([P, MID], F32, name="residual_%d" % i)
+            nc.vector.tensor_tensor(
+                out=residual_i[:].rearrange("p (g t j) -> p g t j", g=MID_PASSES, t=PACK),
+                in0=res1_raw[:].rearrange("p (g j t) -> p g t j", g=MID_PASSES, t=PACK),
+                in1=bias_f2_all[:].rearrange("p (g t j) -> p g t j", g=MID_PASSES, t=PACK),
+                op=ALU.add,
+            )
+            residual.append(residual_i)
+
+        scales_by_row = w_f2_scales.bitcast(I32).rearrange("(a b) q n -> q b a n", b=PLANES_PER_TILE)
+        for quadrant in range(4):
+            for r in range(4):
+                first = 32 * quadrant + r
+                nc.sync.dma_start(
+                    out=w_planes[first : first + 4 * PLANES_PER_TILE : 4, :, :].bitcast(I32),
+                    in_=scales_by_row[4 * quadrant + r],
+                )
+
+        acc = [
+            [psum_acc.tile([P, BANK], F32, name="acc_%d_%d" % (i, n)) for n in range(MID // BANK)]
+            for i in range(TOKEN_TILES)
+        ]
+        words_by_pass = w_f2_words.rearrange("g p n t -> g p (n t)").bitcast(I32)
+        for chunk in range(FFN_PASSES // W_CHUNK_PASSES):
+            w_words = w_stream.tile([P, W_CHUNK_PASSES, MID], U32, name="w_words", align_bytes=64)
+            g0 = chunk * W_CHUNK_PASSES
+            nc.sync.dma_start(
+                out=w_words[:].bitcast(I32),
+                in_=words_by_pass[g0 : g0 + W_CHUNK_PASSES].rearrange("g p n -> p g n"),
+            )
+            for g_in_chunk in range(W_CHUNK_PASSES):
+                g = g0 + g_in_chunk
+                block, offset = g // PLANES_PER_TILE, 4 * (g % PLANES_PER_TILE)
+                for i in range(TOKEN_TILES):
+                    for n in range(MID // BANK):
+                        n_cols = slice(n * BANK, (n + 1) * BANK)
+                        nc.tensor.matmul_mx(
+                            out=acc[i][n][:],
+                            lhsT=h_codes[:, i, g, :].bitcast(FP8X4),
+                            lhsT_scale=h_scales[:, i, g, :],
+                            rhs=w_words[:, g_in_chunk, n_cols].bitcast(FP8X4),
+                            rhs_scale=w_planes[offset:P, block, n_cols],
+                            start=(g == 0),
+                            stop=(g == FFN_PASSES - 1),
+                        )
+
+        wh_words = keep.tile([P, MID_PASSES, D_OUT], U32, name="wh_words", align_bytes=64)
+        nc.sync.dma_start(
+            out=wh_words[:].bitcast(I32),
+            in_=w_h_words.rearrange("g p n t -> g p (n t)").bitcast(I32).rearrange("g p n -> p g n"),
+        )
+        for quadrant in range(4):
+            nc.sync.dma_start(
+                out=wh_planes[32 * quadrant : 32 * quadrant + 4, :, :].bitcast(I32),
+                in_=w_h_scales.bitcast(I32)[:, 4 * quadrant : 4 * quadrant + 4, :].rearrange("g q n -> q g n"),
+            )
+
+        tail = stack.enter_context(tc.tile_pool(name="tail", bufs=2))
+        for i in range(TOKEN_TILES):
+            res2 = tail.tile([P, MID], F32, name="res2")
+            row_sums = tail.tile([P, MID_PASSES], F32, name="row_sums")
+            for g in range(MID_PASSES):
+                g_cols = slice(g * BANK, (g + 1) * BANK)
+                nc.vector.scalar_tensor_tensor(
+                    out=as_t_j(res2[:, g_cols]),
+                    in0=word_order(acc[i][g][:]),
+                    scalar=1.0,
+                    in1=as_t_j(residual[i][:, g_cols]),
+                    op0=ALU.mult,
+                    op1=ALU.add,
+                    accum_out=row_sums[:, g : g + 1],
+                )
+            neg_mean = tail.tile([P, 1], F32, name="neg_mean")
+            nc.vector.tensor_scalar(
+                out=neg_mean[:],
+                in0=row_sums[:, 0:1],
+                scalar1=row_sums[:, 1:2],
+                scalar2=-1.0 / MID,
+                op0=ALU.add,
+                op1=ALU.mult,
+            )
+            squares = tail.tile([P, MID], BF16, name="squares")
+            square_sum = tail.tile([P, 1], F32, name="square_sum")
+            nc.scalar.activation(
+                out=squares[:], in_=res2[:], func=ACT.Square, bias=neg_mean[:], scale=1.0,
+                accum_out=square_sum[:],
+            )
+            std = tail.tile([P, 1], F32, name="std")
+            nc.scalar.activation(
+                out=std[:], in_=square_sum[:], func=ACT.Sqrt, bias=eps[:], scale=1.0 / MID
+            )
+            rstd = tail.tile([P, 1], F32, name="rstd")
+            nc.vector.reciprocal(out=rstd[:], in_=std[:])
+            gained = tail.tile([P, MID], F32, name="gained")
+            nc.vector.scalar_tensor_tensor(
+                out=gained[:], in0=res2[:], scalar=neg_mean[:], in1=gain_all[:],
+                op0=ALU.add, op1=ALU.mult,
+            )
+            norm2 = tail.tile([P, MID], BF16, name="norm2")
+            nc.vector.scalar_tensor_tensor(
+                out=norm2[:], in0=gained[:], scalar=rstd[:], in1=shift_all[:],
+                op0=ALU.mult, op1=ALU.add,
+            )
+            norm_grouped = tail.tile([P, MID_PASSES, P, PACK], BF16, name="norm_grouped", align_bytes=64)
+            for g in range(MID_PASSES):
+                norm_turned = psum_work.tile([P, PACK, P], BF16, name="norm_turned", tag="work")
+                for t in range(PACK):
+                    first = (g * PACK + t) * P
+                    nc.tensor.transpose(norm_turned[:, t, :], norm2[:, first : first + P], ident_bf16[:])
+                nc.scalar.copy(out=norm_grouped[:, g], in_=norm_turned[:].rearrange("p t r -> p r t"))
+            norm_codes = tail.tile([P, MID_PASSES, P], U32, name="norm_codes", align_bytes=64)
+            norm_scales = tail.tile([P, MID_PASSES, P], U8, name="norm_scales", align_bytes=64)
+            nc.vector.quantize_mx(
+                out=norm_codes[:].rearrange("p g r -> p (g r)").bitcast(FP8X4),
+                scales=norm_scales[:].rearrange("p g r -> p (g r)"),
+                in_=norm_grouped[:].rearrange("p g r t -> p (g r t)"),
+            )
+            head = psum_work.tile([P, D_OUT], F32, name="head", tag="work")
+            for g in range(MID_PASSES):
+                nc.tensor.matmul_mx(
+                    out=head[:],
+                    lhsT=norm_codes[:, g, :].bitcast(FP8X4),
+                    lhsT_scale=norm_scales[:, g, :],
+                    rhs=wh_words[:, g, :].bitcast(FP8X4),
+                    rhs_scale=wh_planes[:, g, :],
+                    start=(g == 0),
+                    stop=(g == MID_PASSES - 1),
+                )
+            result = tail.tile([P, D_OUT], F32, name="result")
+            nc.vector.tensor_tensor(out=result[:], in0=head[:], in1=bias_h_all[:], op=ALU.add)
+            nc.sync.dma_start(out=out[i], in_=result[:])

@@ -55,8 +55,6 @@ def tile_tsh_mid_block_pb_k_kernel(
 
         ident_f32 = keep.tile([P, P], F32, name="ident_f32")
         make_identity(nc, ident_f32[:])
-        ident_bf16 = keep.tile([P, P], BF16, name="ident_bf16")
-        make_identity(nc, ident_bf16[:])
         ones = keep.tile([P, P], BF16, name="ones")
         nc.vector.memset(ones[:], 1.0)
         eps = keep.tile([P, 1], F32, name="eps")
@@ -70,6 +68,18 @@ def tile_tsh_mid_block_pb_k_kernel(
         nc.vector.memset(w_planes[:].bitcast(I32), 0)
         wh_planes = keep.tile([P, MID_PASSES, D_OUT], U8, name="wh_planes", align_bytes=64)
         nc.vector.memset(wh_planes[:].bitcast(I32), 0)
+
+        scales_by_row = w_f2_scales.bitcast(F32).rearrange("(a b) q n -> q b a n", b=PLANES_PER_TILE)
+        for quadrant in range(4):
+            for r in range(4):
+                first = 32 * quadrant + r
+                nc.gpsimd.dma_start(
+                    out=w_planes[first : first + 4 * PLANES_PER_TILE : 4, :, :].bitcast(F32),
+                    in_=scales_by_row[4 * quadrant + r],
+                )
+
+        ident_bf16 = keep.tile([P, P], BF16, name="ident_bf16")
+        make_identity(nc, ident_bf16[:])
 
         h_codes = keep.tile([P, TOKEN_TILES, FFN_PASSES, P], U32, name="h_codes", align_bytes=64)
         h_scales = keep.tile([P, TOKEN_TILES, FFN_PASSES, P], U8, name="h_scales", align_bytes=64)
@@ -172,15 +182,6 @@ def tile_tsh_mid_block_pb_k_kernel(
                 op=ALU.add,
             )
             residual.append(residual_i)
-
-        scales_by_row = w_f2_scales.bitcast(I32).rearrange("(a b) q n -> q b a n", b=PLANES_PER_TILE)
-        for quadrant in range(4):
-            for r in range(4):
-                first = 32 * quadrant + r
-                nc.sync.dma_start(
-                    out=w_planes[first : first + 4 * PLANES_PER_TILE : 4, :, :].bitcast(I32),
-                    in_=scales_by_row[4 * quadrant + r],
-                )
 
         acc = [
             [psum_acc.tile([P, BANK], F32, name="acc_%d_%d" % (i, n)) for n in range(MID // BANK)]

@@ -31,6 +31,8 @@ BANK_PASSES = 2
 W_CHUNK_PASSES = 2
 W_BUFS = 7
 PLANES_PER_TILE = 4
+PLANE_BLOCKS = FFN_PASSES // PLANES_PER_TILE
+SYNC_PLANE_BLOCKS = 2
 
 FLOPS = 2 * TOKEN_TILES * P * (FFN * MID + MID * D_OUT)
 
@@ -62,21 +64,21 @@ def tile_tsh_mid_block_pb_k_kernel(
         table_warm = keep.tile([P, 1], F32, name="table_warm")
         nc.scalar.activation(out=table_warm[:], in_=eps[:], func=ACT.Sqrt)
 
-        w_planes = keep.tile(
-            [P, FFN_PASSES // PLANES_PER_TILE, MID], U8, name="w_planes", align_bytes=64
-        )
+        w_planes = keep.tile([P, PLANE_BLOCKS, MID], U8, name="w_planes", align_bytes=64)
         nc.vector.memset(w_planes[:].bitcast(I32), 0)
         wh_planes = keep.tile([P, MID_PASSES, D_OUT], U8, name="wh_planes", align_bytes=64)
         nc.vector.memset(wh_planes[:].bitcast(I32), 0)
 
-        scales_by_row = w_f2_scales.bitcast(F32).rearrange("(a b) q n -> q b a n", b=PLANES_PER_TILE)
-        for quadrant in range(4):
-            for r in range(4):
-                first = 32 * quadrant + r
-                nc.gpsimd.dma_start(
-                    out=w_planes[first : first + 4 * PLANES_PER_TILE : 4, :, :].bitcast(F32),
-                    in_=scales_by_row[4 * quadrant + r],
+        def load_scale_block(queue, word, block):
+            passes = slice(block * PLANES_PER_TILE, (block + 1) * PLANES_PER_TILE)
+            for quadrant in range(4):
+                queue.dma_start(
+                    out=w_planes[32 * quadrant : 32 * quadrant + 16, block, :].bitcast(word),
+                    in_=w_f2_scales.bitcast(word)[passes, 4 * quadrant : 4 * quadrant + 4, :],
                 )
+
+        for block in range(SYNC_PLANE_BLOCKS, PLANE_BLOCKS):
+            load_scale_block(nc.gpsimd, F32, block)
 
         ident_bf16 = keep.tile([P, P], BF16, name="ident_bf16")
         make_identity(nc, ident_bf16[:])
@@ -182,6 +184,9 @@ def tile_tsh_mid_block_pb_k_kernel(
                 op=ALU.add,
             )
             residual.append(residual_i)
+
+        for block in range(SYNC_PLANE_BLOCKS):
+            load_scale_block(nc.sync, I32, block)
 
         acc = [
             [psum_acc.tile([P, BANK], F32, name="acc_%d_%d" % (i, n)) for n in range(MID // BANK)]

@@ -200,12 +200,12 @@ def tile_tsh_mid_block_pb_k_kernel(
                 out=w_words[:].bitcast(I32),
                 in_=words_by_pass[g0 : g0 + W_CHUNK_PASSES].rearrange("g p n -> p g n"),
             )
-            for g_in_chunk in range(W_CHUNK_PASSES):
-                g = g0 + g_in_chunk
-                block, offset = g // PLANES_PER_TILE, 4 * (g % PLANES_PER_TILE)
-                for i in range(TOKEN_TILES):
-                    for n in range(MID // BANK):
-                        n_cols = slice(n * BANK, (n + 1) * BANK)
+            for i in range(TOKEN_TILES):
+                for n in range(MID // BANK):
+                    n_cols = slice(n * BANK, (n + 1) * BANK)
+                    for g_in_chunk in range(W_CHUNK_PASSES):
+                        g = g0 + g_in_chunk
+                        block, offset = g // PLANES_PER_TILE, 4 * (g % PLANES_PER_TILE)
                         nc.tensor.matmul_mx(
                             out=acc[i][n][:],
                             lhsT=h_codes[:, i, g, :].bitcast(FP8X4),
@@ -227,77 +227,101 @@ def tile_tsh_mid_block_pb_k_kernel(
                 in_=w_h_scales.bitcast(I32)[:, 4 * quadrant : 4 * quadrant + 4, :].rearrange("g q n -> q g n"),
             )
 
-        tail = stack.enter_context(tc.tile_pool(name="tail", bufs=2))
-        for i in range(TOKEN_TILES):
-            res2 = tail.tile([P, MID], F32, name="res2")
-            row_sums = tail.tile([P, MID_PASSES], F32, name="row_sums")
-            for g in range(MID_PASSES):
-                g_cols = slice(g * BANK, (g + 1) * BANK)
-                nc.vector.scalar_tensor_tensor(
-                    out=as_t_j(res2[:, g_cols]),
-                    in0=word_order(acc[i][g][:]),
-                    scalar=1.0,
-                    in1=as_t_j(residual[i][:, g_cols]),
-                    op0=ALU.mult,
-                    op1=ALU.add,
-                    accum_out=row_sums[:, g : g + 1],
+        tail = stack.enter_context(tc.tile_pool(name="tail", bufs=1))
+
+        def per_tile(shape, dtype, name, **options):
+            return [
+                tail.tile(shape, dtype, name="%s_%d" % (name, i), **options) for i in range(TOKEN_TILES)
+            ]
+
+        def half(columns, g):
+            return columns[:, g * BANK : (g + 1) * BANK]
+
+        res2 = per_tile([P, MID], F32, "res2")
+        row_sums = per_tile([P, MID_PASSES], F32, "row_sums")
+        neg_mean = per_tile([P, 1], F32, "neg_mean")
+        squares = per_tile([P, MID], BF16, "squares")
+        square_sum = per_tile([P, 1], F32, "square_sum")
+        std = per_tile([P, 1], F32, "std")
+        rstd = per_tile([P, 1], F32, "rstd")
+        gained = per_tile([P, MID], F32, "gained")
+        norm2 = per_tile([P, MID], BF16, "norm2")
+        norm_grouped = per_tile([P, MID_PASSES, P, PACK], BF16, "norm_grouped", align_bytes=64)
+        norm_codes = per_tile([P, MID_PASSES, P], U32, "norm_codes", align_bytes=64)
+        norm_scales = per_tile([P, MID_PASSES, P], U8, "norm_scales", align_bytes=64)
+        result = per_tile([P, D_OUT], F32, "result")
+
+        with tc.manual_schedule():
+            for i in range(TOKEN_TILES):
+                for g in range(MID_PASSES):
+                    nc.vector.scalar_tensor_tensor(
+                        out=as_t_j(half(res2[i], g)),
+                        in0=word_order(acc[i][g][:]),
+                        scalar=1.0,
+                        in1=as_t_j(half(residual[i], g)),
+                        op0=ALU.mult,
+                        op1=ALU.add,
+                        accum_out=row_sums[i][:, g : g + 1],
+                    )
+                nc.vector.tensor_scalar(
+                    out=neg_mean[i][:],
+                    in0=row_sums[i][:, 0:1],
+                    scalar1=row_sums[i][:, 1:2],
+                    scalar2=-1.0 / MID,
+                    op0=ALU.add,
+                    op1=ALU.mult,
                 )
-            neg_mean = tail.tile([P, 1], F32, name="neg_mean")
-            nc.vector.tensor_scalar(
-                out=neg_mean[:],
-                in0=row_sums[:, 0:1],
-                scalar1=row_sums[:, 1:2],
-                scalar2=-1.0 / MID,
-                op0=ALU.add,
-                op1=ALU.mult,
-            )
-            squares = tail.tile([P, MID], BF16, name="squares")
-            square_sum = tail.tile([P, 1], F32, name="square_sum")
-            nc.scalar.activation(
-                out=squares[:], in_=res2[:], func=ACT.Square, bias=neg_mean[:], scale=1.0,
-                accum_out=square_sum[:],
-            )
-            std = tail.tile([P, 1], F32, name="std")
-            nc.scalar.activation(
-                out=std[:], in_=square_sum[:], func=ACT.Sqrt, bias=eps[:], scale=1.0 / MID
-            )
-            rstd = tail.tile([P, 1], F32, name="rstd")
-            nc.vector.reciprocal(out=rstd[:], in_=std[:])
-            gained = tail.tile([P, MID], F32, name="gained")
-            nc.vector.scalar_tensor_tensor(
-                out=gained[:], in0=res2[:], scalar=neg_mean[:], in1=gain_all[:],
-                op0=ALU.add, op1=ALU.mult,
-            )
-            norm2 = tail.tile([P, MID], BF16, name="norm2")
-            nc.vector.scalar_tensor_tensor(
-                out=norm2[:], in0=gained[:], scalar=rstd[:], in1=shift_all[:],
-                op0=ALU.mult, op1=ALU.add,
-            )
-            norm_grouped = tail.tile([P, MID_PASSES, P, PACK], BF16, name="norm_grouped", align_bytes=64)
-            for g in range(MID_PASSES):
-                norm_turned = psum_work.tile([P, PACK, P], BF16, name="norm_turned", tag="work")
-                for t in range(PACK):
-                    first = (g * PACK + t) * P
-                    nc.tensor.transpose(norm_turned[:, t, :], norm2[:, first : first + P], ident_bf16[:])
-                nc.scalar.copy(out=norm_grouped[:, g], in_=norm_turned[:].rearrange("p t r -> p r t"))
-            norm_codes = tail.tile([P, MID_PASSES, P], U32, name="norm_codes", align_bytes=64)
-            norm_scales = tail.tile([P, MID_PASSES, P], U8, name="norm_scales", align_bytes=64)
-            nc.vector.quantize_mx(
-                out=norm_codes[:].rearrange("p g r -> p (g r)").bitcast(FP8X4),
-                scales=norm_scales[:].rearrange("p g r -> p (g r)"),
-                in_=norm_grouped[:].rearrange("p g r t -> p (g r t)"),
-            )
-            head = psum_work.tile([P, D_OUT], F32, name="head", tag="work")
-            for g in range(MID_PASSES):
-                nc.tensor.matmul_mx(
-                    out=head[:],
-                    lhsT=norm_codes[:, g, :].bitcast(FP8X4),
-                    lhsT_scale=norm_scales[:, g, :],
-                    rhs=wh_words[:, g, :].bitcast(FP8X4),
-                    rhs_scale=wh_planes[:, g, :],
-                    start=(g == 0),
-                    stop=(g == MID_PASSES - 1),
+                nc.scalar.activation(
+                    out=squares[i][:], in_=res2[i][:], func=ACT.Square, bias=neg_mean[i][:], scale=1.0,
+                    accum_out=square_sum[i][:],
                 )
-            result = tail.tile([P, D_OUT], F32, name="result")
-            nc.vector.tensor_tensor(out=result[:], in0=head[:], in1=bias_h_all[:], op=ALU.add)
-            nc.sync.dma_start(out=out[i], in_=result[:])
+                nc.scalar.activation(
+                    out=std[i][:], in_=square_sum[i][:], func=ACT.Sqrt, bias=eps[:], scale=1.0 / MID
+                )
+
+            for i in range(TOKEN_TILES):
+                for g in range(MID_PASSES):
+                    nc.vector.scalar_tensor_tensor(
+                        out=half(gained[i], g), in0=half(res2[i], g), scalar=neg_mean[i][:],
+                        in1=half(gain_all, g), op0=ALU.add, op1=ALU.mult,
+                    )
+
+            for i in range(TOKEN_TILES):
+                nc.vector.reciprocal(out=rstd[i][:], in_=std[i][:])
+                for g in range(MID_PASSES):
+                    nc.vector.scalar_tensor_tensor(
+                        out=half(norm2[i], g), in0=half(gained[i], g), scalar=rstd[i][:],
+                        in1=half(shift_all, g), op0=ALU.mult, op1=ALU.add,
+                    )
+                    norm_turned = psum_work.tile([P, PACK, P], BF16, name="norm_turned", tag="work")
+                    for t in range(PACK):
+                        first = (g * PACK + t) * P
+                        nc.tensor.transpose(
+                            norm_turned[:, t, :], norm2[i][:, first : first + P], ident_bf16[:]
+                        )
+                    nc.scalar.copy(
+                        out=norm_grouped[i][:, g], in_=norm_turned[:].rearrange("p t r -> p r t")
+                    )
+
+            head = []
+            for i in range(TOKEN_TILES):
+                head.append(psum_work.tile([P, D_OUT], F32, name="head_%d" % i, tag="work"))
+                for g in range(MID_PASSES):
+                    nc.vector.quantize_mx(
+                        out=norm_codes[i][:, g, :].bitcast(FP8X4),
+                        scales=norm_scales[i][:, g, :],
+                        in_=norm_grouped[i][:, g].rearrange("p r t -> p (r t)"),
+                    )
+                    nc.tensor.matmul_mx(
+                        out=head[i][:],
+                        lhsT=norm_codes[i][:, g, :].bitcast(FP8X4),
+                        lhsT_scale=norm_scales[i][:, g, :],
+                        rhs=wh_words[:, g, :].bitcast(FP8X4),
+                        rhs_scale=wh_planes[:, g, :],
+                        start=(g == 0),
+                        stop=(g == MID_PASSES - 1),
+                    )
+
+            for i in range(TOKEN_TILES):
+                nc.vector.tensor_tensor(out=result[i][:], in0=head[i][:], in1=bias_h_all[:], op=ALU.add)
+                nc.sync.dma_start(out=out[i], in_=result[i][:])

@@ -52,8 +52,6 @@ def tile_tsh_mid_block_pb_k_kernel(
     with ExitStack() as stack:
         keep = stack.enter_context(tc.tile_pool(name="keep", bufs=1))
         w_stream = stack.enter_context(tc.tile_pool(name="w_stream", bufs=W_BUFS))
-        psum_acc = stack.enter_context(tc.psum_pool(name="psum_acc", bufs=1))
-        psum_work = stack.enter_context(tc.psum_pool(name="psum_work", bufs=4))
 
         ident_f32 = keep.tile([P, P], F32, name="ident_f32")
         make_identity(nc, ident_f32[:])
@@ -96,6 +94,7 @@ def tile_tsh_mid_block_pb_k_kernel(
             )
             stage = part1.enter_context(tc.tile_pool(name="stage", bufs=4))
             rows_pool = part1.enter_context(tc.tile_pool(name="rows", bufs=1))
+            psum_turn = part1.enter_context(tc.psum_pool(name="psum_turn", bufs=8))
 
             vector_rows = rows_pool.tile([P, 3 * MID + D_OUT], BF16, name="vector_rows")
             nc.vector.memset(vector_rows[:].bitcast(I32), 0)
@@ -108,48 +107,53 @@ def tile_tsh_mid_block_pb_k_kernel(
                 out=vector_rows[0:1, 3 * MID :], in_=b_h.rearrange("(o n) -> o n", o=1)
             )
 
-            banks_emptied = 0
-            for chunk in range(FFN_PASSES // H_CHUNK_PASSES):
-                for i in range(TOKEN_TILES):
-                    h_raw = h_pool.tile([P, H_CHUNK_PASSES * K_PASS], BF16, name="h_raw")
-                    first_k = chunk * H_CHUNK_PASSES * K_PASS
-                    nc.sync.dma_start(
-                        out=h_raw[:], in_=h[i, :, first_k : first_k + H_CHUNK_PASSES * K_PASS]
-                    )
-                    h_pairs = h_raw[:].bitcast(F32)
-                    for quarter in range(H_CHUNK_PASSES // QUANT_PASSES):
-                        grouped = stage.tile(
-                            [P, QUANT_PASSES * P * PACK], BF16, name="grouped", align_bytes=64
+            def quantise_h(grouped, i, g0):
+                nc.vector.quantize_mx(
+                    out=h_codes[:, i, g0 : g0 + QUANT_PASSES, :].rearrange("p g r -> p (g r)").bitcast(FP8X4),
+                    scales=h_scales[:, i, g0 : g0 + QUANT_PASSES, :].rearrange("p g r -> p (g r)"),
+                    in_=grouped[:],
+                )
+
+            with tc.manual_schedule():
+                banks_emptied = 0
+                waiting = None
+                for chunk in range(FFN_PASSES // H_CHUNK_PASSES):
+                    for i in range(TOKEN_TILES):
+                        h_raw = h_pool.tile([P, H_CHUNK_PASSES * K_PASS], BF16, name="h_raw")
+                        first_k = chunk * H_CHUNK_PASSES * K_PASS
+                        nc.sync.dma_start(
+                            out=h_raw[:], in_=h[i, :, first_k : first_k + H_CHUNK_PASSES * K_PASS]
                         )
-                        grouped_pairs = grouped[:].bitcast(F32).rearrange(
-                            "p (g r u) -> p g r u", g=QUANT_PASSES, r=P
-                        )
-                        for bank in range(QUANT_PASSES // BANK_PASSES):
-                            turned = psum_work.tile([P, BANK_PASSES, 2, P], F32, name="turned", tag="work")
-                            for g_in_bank in range(BANK_PASSES):
-                                g_in_chunk = quarter * QUANT_PASSES + bank * BANK_PASSES + g_in_bank
-                                first_pair = g_in_chunk * K_PASS // 2
-                                for u in range(2):
-                                    nc.tensor.transpose(
-                                        turned[:, g_in_bank, u, :],
-                                        h_pairs[:, first_pair + u : first_pair + K_PASS // 2 : 2],
-                                        ident_f32[:],
-                                    )
-                            target = grouped_pairs[:, bank * BANK_PASSES : (bank + 1) * BANK_PASSES]
-                            source = turned[:].rearrange("p g u r -> p g r u")
-                            if banks_emptied % 4 == 3:
-                                nc.vector.tensor_copy(out=target, in_=source)
-                            else:
-                                nc.scalar.copy(out=target, in_=source)
-                            banks_emptied += 1
-                        g0 = chunk * H_CHUNK_PASSES + quarter * QUANT_PASSES
-                        nc.vector.quantize_mx(
-                            out=h_codes[:, i, g0 : g0 + QUANT_PASSES, :]
-                            .rearrange("p g r -> p (g r)")
-                            .bitcast(FP8X4),
-                            scales=h_scales[:, i, g0 : g0 + QUANT_PASSES, :].rearrange("p g r -> p (g r)"),
-                            in_=grouped[:],
-                        )
+                        h_pairs = h_raw[:].bitcast(F32)
+                        for quarter in range(H_CHUNK_PASSES // QUANT_PASSES):
+                            grouped = stage.tile(
+                                [P, QUANT_PASSES * P * PACK], BF16, name="grouped", align_bytes=64
+                            )
+                            grouped_pairs = grouped[:].bitcast(F32).rearrange(
+                                "p (g r u) -> p g r u", g=QUANT_PASSES, r=P
+                            )
+                            for bank in range(QUANT_PASSES // BANK_PASSES):
+                                turned = psum_turn.tile([P, BANK_PASSES, 2, P], F32, name="turned", tag="work")
+                                for g_in_bank in range(BANK_PASSES):
+                                    g_in_chunk = quarter * QUANT_PASSES + bank * BANK_PASSES + g_in_bank
+                                    first_pair = g_in_chunk * K_PASS // 2
+                                    for u in range(2):
+                                        nc.tensor.transpose(
+                                            turned[:, g_in_bank, u, :],
+                                            h_pairs[:, first_pair + u : first_pair + K_PASS // 2 : 2],
+                                            ident_f32[:],
+                                        )
+                                target = grouped_pairs[:, bank * BANK_PASSES : (bank + 1) * BANK_PASSES]
+                                source = turned[:].rearrange("p g u r -> p g r u")
+                                if banks_emptied % 4 == 3:
+                                    nc.vector.tensor_copy(out=target, in_=source)
+                                else:
+                                    nc.scalar.copy(out=target, in_=source)
+                                banks_emptied += 1
+                            if waiting is not None:
+                                quantise_h(*waiting)
+                            waiting = (grouped, i, chunk * H_CHUNK_PASSES + quarter * QUANT_PASSES)
+                quantise_h(*waiting)
 
             spread_targets = (
                 [as_t_j(bias_f2_all[:, g * BANK : (g + 1) * BANK]) for g in range(MID_PASSES)]
@@ -157,7 +161,7 @@ def tile_tsh_mid_block_pb_k_kernel(
                 + [as_t_j(shift_all[:, g * BANK : (g + 1) * BANK]) for g in range(MID_PASSES)]
             )
             for position, target in enumerate(spread_targets):
-                spread = psum_work.tile([P, BANK], F32, name="spread", tag="work")
+                spread = psum_turn.tile([P, BANK], F32, name="spread", tag="work")
                 nc.tensor.matmul(
                     out=spread[:],
                     lhsT=ones[:],
@@ -166,7 +170,7 @@ def tile_tsh_mid_block_pb_k_kernel(
                     stop=True,
                 )
                 nc.scalar.copy(out=target, in_=word_order(spread[:]))
-            spread = psum_work.tile([P, BANK], F32, name="spread", tag="work")
+            spread = psum_turn.tile([P, BANK], F32, name="spread", tag="work")
             nc.tensor.matmul(
                 out=spread[:], lhsT=ones[:], rhs=vector_rows[:, 3 * MID :], start=True, stop=True
             )
@@ -188,6 +192,8 @@ def tile_tsh_mid_block_pb_k_kernel(
         for block in range(SYNC_PLANE_BLOCKS):
             load_scale_block(nc.sync, I32, block)
 
+        psum_acc = stack.enter_context(tc.psum_pool(name="psum_acc", bufs=1, reuse_waits="tile"))
+        psum_work = stack.enter_context(tc.psum_pool(name="psum_work", bufs=4, reuse_waits="tile"))
         acc = [
             [psum_acc.tile([P, BANK], F32, name="acc_%d_%d" % (i, n)) for n in range(MID // BANK)]
             for i in range(TOKEN_TILES)

@@ -32,7 +32,7 @@ W_CHUNK_PASSES = 2
 W_BUFS = 7
 PLANES_PER_TILE = 4
 PLANE_BLOCKS = FFN_PASSES // PLANES_PER_TILE
-SYNC_PLANE_BLOCKS = 2
+SYNC_PLANE_BLOCKS = 0
 
 FLOPS = 2 * TOKEN_TILES * P * (FFN * MID + MID * D_OUT)
 

@@ -60,7 +60,7 @@ def tile_tsh_mid_block_pb_k_kernel(
         eps = keep.tile([P, 1], F32, name="eps")
         nc.vector.memset(eps[:], LN_EPS)
         table_warm = keep.tile([P, 1], F32, name="table_warm")
-        nc.scalar.activation(out=table_warm[:], in_=eps[:], func=ACT.Sqrt)
+        nc.scalar.activation(out=table_warm[:], in_=eps[:], func=ACT.Abs_reciprocal_sqrt)
 
         w_planes = keep.tile([P, PLANE_BLOCKS, MID], U8, name="w_planes", align_bytes=64)
         nc.vector.memset(w_planes[:].bitcast(I32), 0)
@@ -248,7 +248,6 @@ def tile_tsh_mid_block_pb_k_kernel(
         neg_mean = per_tile([P, 1], F32, "neg_mean")
         squares = per_tile([P, MID], BF16, "squares")
         square_sum = per_tile([P, 1], F32, "square_sum")
-        std = per_tile([P, 1], F32, "std")
         rstd = per_tile([P, 1], F32, "rstd")
         gained = per_tile([P, MID], F32, "gained")
         norm2 = per_tile([P, MID], BF16, "norm2")
@@ -257,43 +256,53 @@ def tile_tsh_mid_block_pb_k_kernel(
         norm_scales = per_tile([P, MID_PASSES, P], U8, "norm_scales", align_bytes=64)
         result = per_tile([P, D_OUT], F32, "result")
 
+        def empty_bank(i, g):
+            nc.vector.scalar_tensor_tensor(
+                out=as_t_j(half(res2[i], g)),
+                in0=word_order(acc[i][g][:]),
+                scalar=1.0,
+                in1=as_t_j(half(residual[i], g)),
+                op0=ALU.mult,
+                op1=ALU.add,
+                accum_out=row_sums[i][:, g : g + 1],
+            )
+
+        def statistics(i):
+            nc.vector.tensor_scalar(
+                out=neg_mean[i][:],
+                in0=row_sums[i][:, 0:1],
+                scalar1=row_sums[i][:, 1:2],
+                scalar2=-1.0 / MID,
+                op0=ALU.add,
+                op1=ALU.mult,
+            )
+            nc.scalar.activation(
+                out=squares[i][:], in_=res2[i][:], func=ACT.Square, bias=neg_mean[i][:], scale=1.0,
+                accum_out=square_sum[i][:],
+            )
+            nc.scalar.activation(
+                out=rstd[i][:], in_=square_sum[i][:], func=ACT.Abs_reciprocal_sqrt, bias=eps[:], scale=1.0 / MID
+            )
+
+        def gain(i, g):
+            nc.vector.scalar_tensor_tensor(
+                out=half(gained[i], g), in0=half(res2[i], g), scalar=neg_mean[i][:],
+                in1=half(gain_all, g), op0=ALU.add, op1=ALU.mult,
+            )
+
         with tc.manual_schedule():
-            for i in range(TOKEN_TILES):
-                for g in range(MID_PASSES):
-                    nc.vector.scalar_tensor_tensor(
-                        out=as_t_j(half(res2[i], g)),
-                        in0=word_order(acc[i][g][:]),
-                        scalar=1.0,
-                        in1=as_t_j(half(residual[i], g)),
-                        op0=ALU.mult,
-                        op1=ALU.add,
-                        accum_out=row_sums[i][:, g : g + 1],
-                    )
-                nc.vector.tensor_scalar(
-                    out=neg_mean[i][:],
-                    in0=row_sums[i][:, 0:1],
-                    scalar1=row_sums[i][:, 1:2],
-                    scalar2=-1.0 / MID,
-                    op0=ALU.add,
-                    op1=ALU.mult,
-                )
-                nc.scalar.activation(
-                    out=squares[i][:], in_=res2[i][:], func=ACT.Square, bias=neg_mean[i][:], scale=1.0,
-                    accum_out=square_sum[i][:],
-                )
-                nc.scalar.activation(
-                    out=std[i][:], in_=square_sum[i][:], func=ACT.Sqrt, bias=eps[:], scale=1.0 / MID
-                )
+            empty_bank(0, 0)
+            empty_bank(0, 1)
+            empty_bank(1, 0)
+            statistics(0)
+            empty_bank(1, 1)
+            gain(0, 0)
+            statistics(1)
+            gain(0, 1)
+            gain(1, 0)
+            gain(1, 1)
 
             for i in range(TOKEN_TILES):
-                for g in range(MID_PASSES):
-                    nc.vector.scalar_tensor_tensor(
-                        out=half(gained[i], g), in0=half(res2[i], g), scalar=neg_mean[i][:],
-                        in1=half(gain_all, g), op0=ALU.add, op1=ALU.mult,
-                    )
-
-            for i in range(TOKEN_TILES):
-                nc.vector.reciprocal(out=rstd[i][:], in_=std[i][:])
                 for g in range(MID_PASSES):
                     nc.vector.scalar_tensor_tensor(
                         out=half(norm2[i], g), in0=half(gained[i], g), scalar=rstd[i][:],

@@ -114,6 +114,28 @@ def tile_tsh_mid_block_pb_k_kernel(
                     in_=grouped[:],
                 )
 
+            spread_targets = (
+                [as_t_j(bias_f2_all[:, g * BANK : (g + 1) * BANK]) for g in range(MID_PASSES)]
+                + [as_t_j(gain_all[:, g * BANK : (g + 1) * BANK]) for g in range(MID_PASSES)]
+                + [as_t_j(shift_all[:, g * BANK : (g + 1) * BANK]) for g in range(MID_PASSES)]
+                + [bias_h_all[:]]
+            )
+
+            def spread(position):
+                spread_bank = psum_turn.tile([P, BANK], F32, name="spread_bank", tag="work")
+                nc.tensor.matmul(
+                    out=spread_bank[:],
+                    lhsT=ones[:],
+                    rhs=vector_rows[:, position * BANK : (position + 1) * BANK],
+                    start=True,
+                    stop=True,
+                )
+                source = spread_bank[:] if position == len(spread_targets) - 1 else word_order(spread_bank[:])
+                if position % 2 == 0:
+                    nc.scalar.copy(out=spread_targets[position], in_=source)
+                else:
+                    nc.vector.tensor_copy(out=spread_targets[position], in_=source)
+
             with tc.manual_schedule():
                 banks_emptied = 0
                 waiting = None
@@ -153,33 +175,14 @@ def tile_tsh_mid_block_pb_k_kernel(
                             if waiting is not None:
                                 quantise_h(*waiting)
                             waiting = (grouped, i, chunk * H_CHUNK_PASSES + quarter * QUANT_PASSES)
+                        if chunk * TOKEN_TILES + i < len(spread_targets):
+                            spread(chunk * TOKEN_TILES + i)
                 quantise_h(*waiting)
-
-            spread_targets = (
-                [as_t_j(bias_f2_all[:, g * BANK : (g + 1) * BANK]) for g in range(MID_PASSES)]
-                + [as_t_j(gain_all[:, g * BANK : (g + 1) * BANK]) for g in range(MID_PASSES)]
-                + [as_t_j(shift_all[:, g * BANK : (g + 1) * BANK]) for g in range(MID_PASSES)]
-            )
-            for position, target in enumerate(spread_targets):
-                spread = psum_turn.tile([P, BANK], F32, name="spread", tag="work")
-                nc.tensor.matmul(
-                    out=spread[:],
-                    lhsT=ones[:],
-                    rhs=vector_rows[:, position * BANK : (position + 1) * BANK],
-                    start=True,
-                    stop=True,
-                )
-                nc.scalar.copy(out=target, in_=word_order(spread[:]))
-            spread = psum_turn.tile([P, BANK], F32, name="spread", tag="work")
-            nc.tensor.matmul(
-                out=spread[:], lhsT=ones[:], rhs=vector_rows[:, 3 * MID :], start=True, stop=True
-            )
-            nc.scalar.copy(out=bias_h_all[:], in_=spread[:])
 
         residual = []
         for i in range(TOKEN_TILES):
             res1_raw = keep.tile([P, MID], BF16, name="res1_raw_%d" % i)
-            nc.sync.dma_start(out=res1_raw[:], in_=res1[i])
+            nc.gpsimd.dma_start(out=res1_raw[:], in_=res1[i])
             residual_i = keep.tile([P, MID], F32, name="residual_%d" % i)
             nc.vector.tensor_tensor(
                 out=residual_i[:].rearrange("p (g t j) -> p g t j", g=MID_PASSES, t=PACK),

@@ -295,12 +295,20 @@ def tile_tsh_mid_block_pb_k_kernel(
 
         with tc.manual_schedule():
             empty_bank(0, 0)
+            idle_bank = psum_acc.tile([P, BANK], F32, name="idle_bank", tag="acc_0_0")
+
+            def keep_clock(columns):
+                for g in range(MID_PASSES):
+                    nc.tensor.matmul(out=idle_bank[:], lhsT=ones[:], rhs=half(columns, g), start=True, stop=True)
+
             empty_bank(0, 1)
             empty_bank(1, 0)
             statistics(0)
+            keep_clock(squares[0])
             empty_bank(1, 1)
             gain(0, 0)
             statistics(1)
+            keep_clock(squares[1])
             gain(0, 1)
             gain(1, 0)
             gain(1, 1)
@@ -320,6 +328,8 @@ def tile_tsh_mid_block_pb_k_kernel(
                     nc.scalar.copy(
                         out=norm_grouped[i][:, g], in_=norm_turned[:].rearrange("p t r -> p r t")
                     )
+                    if i == 0 and g == 0:
+                        keep_clock(squares[0])
 
             head = []
             for i in range(TOKEN_TILES):

from contextlib import ExitStack

import concourse.mybir as mybir
from concourse.masks import make_identity

F32 = mybir.dt.float32
BF16 = mybir.dt.bfloat16
I32 = mybir.dt.int32
U32 = mybir.dt.uint32
U8 = mybir.dt.uint8
FP8X4 = mybir.dt.float8_e4m3fn_x4
ALU = mybir.AluOpType
ACT = mybir.ActivationFunctionType

P = 128
PACK = 4
K_PASS = P * PACK
BANK = 512

TOKEN_TILES = 2
FFN = 16384
MID = 1024
D_OUT = 512
LN_EPS = 1e-5
FFN_PASSES = FFN // K_PASS
MID_PASSES = MID // K_PASS

H_CHUNK_PASSES = 8
QUANT_PASSES = 4
BANK_PASSES = 2
W_CHUNK_PASSES = 2
W_BUFS = 7
PLANES_PER_TILE = 4
PLANE_BLOCKS = FFN_PASSES // PLANES_PER_TILE
SYNC_PLANE_BLOCKS = 0

FLOPS = 2 * TOKEN_TILES * P * (FFN * MID + MID * D_OUT)


def word_order(columns):
    return columns.rearrange("p (j t) -> p t j", t=PACK)


def as_t_j(columns):
    return columns.rearrange("p (t j) -> p t j", t=PACK)


def tile_tsh_mid_block_pb_k_kernel(
    tc, h, w_f2_words, w_f2_scales, b_f2, res1, g2, be2, w_h_words, w_h_scales, b_h, out
):
    nc = tc.nc
    with ExitStack() as stack:
        keep = stack.enter_context(tc.tile_pool(name="keep", bufs=1))
        w_stream = stack.enter_context(tc.tile_pool(name="w_stream", bufs=W_BUFS))

        ident_f32 = keep.tile([P, P], F32, name="ident_f32")
        make_identity(nc, ident_f32[:])
        ones = keep.tile([P, P], BF16, name="ones")
        nc.vector.memset(ones[:], 1.0)
        eps = keep.tile([P, 1], F32, name="eps")
        nc.vector.memset(eps[:], LN_EPS)
        table_warm = keep.tile([P, 1], F32, name="table_warm")
        nc.scalar.activation(out=table_warm[:], in_=eps[:], func=ACT.Abs_reciprocal_sqrt)

        w_planes = keep.tile([P, PLANE_BLOCKS, MID], U8, name="w_planes", align_bytes=64)
        nc.vector.memset(w_planes[:].bitcast(I32), 0)
        wh_planes = keep.tile([P, MID_PASSES, D_OUT], U8, name="wh_planes", align_bytes=64)
        nc.vector.memset(wh_planes[:].bitcast(I32), 0)

        def load_scale_block(queue, word, block):
            passes = slice(block * PLANES_PER_TILE, (block + 1) * PLANES_PER_TILE)
            for quadrant in range(4):
                queue.dma_start(
                    out=w_planes[32 * quadrant : 32 * quadrant + 16, block, :].bitcast(word),
                    in_=w_f2_scales.bitcast(word)[passes, 4 * quadrant : 4 * quadrant + 4, :],
                )

        for block in range(SYNC_PLANE_BLOCKS, PLANE_BLOCKS):
            load_scale_block(nc.gpsimd, F32, block)

        ident_bf16 = keep.tile([P, P], BF16, name="ident_bf16")
        make_identity(nc, ident_bf16[:])

        h_codes = keep.tile([P, TOKEN_TILES, FFN_PASSES, P], U32, name="h_codes", align_bytes=64)
        h_scales = keep.tile([P, TOKEN_TILES, FFN_PASSES, P], U8, name="h_scales", align_bytes=64)
        bias_f2_all = keep.tile([P, MID], F32, name="bias_f2_all")
        gain_all = keep.tile([P, MID], F32, name="gain_all")
        shift_all = keep.tile([P, MID], F32, name="shift_all")
        bias_h_all = keep.tile([P, D_OUT], F32, name="bias_h_all")

        with ExitStack() as part1:
            h_pool = part1.enter_context(
                tc.tile_pool(name="h_raw", bufs=TOKEN_TILES * FFN_PASSES // H_CHUNK_PASSES)
            )
            stage = part1.enter_context(tc.tile_pool(name="stage", bufs=4))
            rows_pool = part1.enter_context(tc.tile_pool(name="rows", bufs=1))
            psum_turn = part1.enter_context(tc.psum_pool(name="psum_turn", bufs=8))

            vector_rows = rows_pool.tile([P, 3 * MID + D_OUT], BF16, name="vector_rows")
            nc.vector.memset(vector_rows[:].bitcast(I32), 0)
            for position, vector in enumerate((b_f2, g2, be2)):
                nc.scalar.dma_start(
                    out=vector_rows[0:1, position * MID : (position + 1) * MID],
                    in_=vector.rearrange("(o n) -> o n", o=1),
                )
            nc.scalar.dma_start(
                out=vector_rows[0:1, 3 * MID :], in_=b_h.rearrange("(o n) -> o n", o=1)
            )

            def quantise_h(grouped, i, g0):
                nc.vector.quantize_mx(
                    out=h_codes[:, i, g0 : g0 + QUANT_PASSES, :].rearrange("p g r -> p (g r)").bitcast(FP8X4),
                    scales=h_scales[:, i, g0 : g0 + QUANT_PASSES, :].rearrange("p g r -> p (g r)"),
                    in_=grouped[:],
                )

            spread_targets = (
                [as_t_j(bias_f2_all[:, g * BANK : (g + 1) * BANK]) for g in range(MID_PASSES)]
                + [as_t_j(gain_all[:, g * BANK : (g + 1) * BANK]) for g in range(MID_PASSES)]
                + [as_t_j(shift_all[:, g * BANK : (g + 1) * BANK]) for g in range(MID_PASSES)]
                + [bias_h_all[:]]
            )

            def spread(position):
                spread_bank = psum_turn.tile([P, BANK], F32, name="spread_bank", tag="work")
                nc.tensor.matmul(
                    out=spread_bank[:],
                    lhsT=ones[:],
                    rhs=vector_rows[:, position * BANK : (position + 1) * BANK],
                    start=True,
                    stop=True,
                )
                source = spread_bank[:] if position == len(spread_targets) - 1 else word_order(spread_bank[:])
                if position % 2 == 0:
                    nc.scalar.copy(out=spread_targets[position], in_=source)
                else:
                    nc.vector.tensor_copy(out=spread_targets[position], in_=source)

            with tc.manual_schedule():
                banks_emptied = 0
                waiting = None
                for chunk in range(FFN_PASSES // H_CHUNK_PASSES):
                    for i in range(TOKEN_TILES):
                        h_raw = h_pool.tile([P, H_CHUNK_PASSES * K_PASS], BF16, name="h_raw")
                        first_k = chunk * H_CHUNK_PASSES * K_PASS
                        nc.sync.dma_start(
                            out=h_raw[:], in_=h[i, :, first_k : first_k + H_CHUNK_PASSES * K_PASS]
                        )
                        h_pairs = h_raw[:].bitcast(F32)
                        for quarter in range(H_CHUNK_PASSES // QUANT_PASSES):
                            grouped = stage.tile(
                                [P, QUANT_PASSES * P * PACK], BF16, name="grouped", align_bytes=64
                            )
                            grouped_pairs = grouped[:].bitcast(F32).rearrange(
                                "p (g r u) -> p g r u", g=QUANT_PASSES, r=P
                            )
                            for bank in range(QUANT_PASSES // BANK_PASSES):
                                turned = psum_turn.tile([P, BANK_PASSES, 2, P], F32, name="turned", tag="work")
                                for g_in_bank in range(BANK_PASSES):
                                    g_in_chunk = quarter * QUANT_PASSES + bank * BANK_PASSES + g_in_bank
                                    first_pair = g_in_chunk * K_PASS // 2
                                    for u in range(2):
                                        nc.tensor.transpose(
                                            turned[:, g_in_bank, u, :],
                                            h_pairs[:, first_pair + u : first_pair + K_PASS // 2 : 2],
                                            ident_f32[:],
                                        )
                                target = grouped_pairs[:, bank * BANK_PASSES : (bank + 1) * BANK_PASSES]
                                source = turned[:].rearrange("p g u r -> p g r u")
                                if banks_emptied % 4 == 3:
                                    nc.vector.tensor_copy(out=target, in_=source)
                                else:
                                    nc.scalar.copy(out=target, in_=source)
                                banks_emptied += 1
                            if waiting is not None:
                                quantise_h(*waiting)
                            waiting = (grouped, i, chunk * H_CHUNK_PASSES + quarter * QUANT_PASSES)
                        if chunk * TOKEN_TILES + i < len(spread_targets):
                            spread(chunk * TOKEN_TILES + i)
                quantise_h(*waiting)

        residual = []
        for i in range(TOKEN_TILES):
            res1_raw = keep.tile([P, MID], BF16, name="res1_raw_%d" % i)
            nc.gpsimd.dma_start(out=res1_raw[:], in_=res1[i])
            residual_i = keep.tile([P, MID], F32, name="residual_%d" % i)
            nc.vector.tensor_tensor(
                out=residual_i[:].rearrange("p (g t j) -> p g t j", g=MID_PASSES, t=PACK),
                in0=res1_raw[:].rearrange("p (g j t) -> p g t j", g=MID_PASSES, t=PACK),
                in1=bias_f2_all[:].rearrange("p (g t j) -> p g t j", g=MID_PASSES, t=PACK),
                op=ALU.add,
            )
            residual.append(residual_i)

        for block in range(SYNC_PLANE_BLOCKS):
            load_scale_block(nc.sync, I32, block)

        psum_acc = stack.enter_context(tc.psum_pool(name="psum_acc", bufs=1, reuse_waits="tile"))
        psum_work = stack.enter_context(tc.psum_pool(name="psum_work", bufs=4, reuse_waits="tile"))
        acc = [
            [psum_acc.tile([P, BANK], F32, name="acc_%d_%d" % (i, n)) for n in range(MID // BANK)]
            for i in range(TOKEN_TILES)
        ]
        words_by_pass = w_f2_words.rearrange("g p n t -> g p (n t)").bitcast(I32)
        for chunk in range(FFN_PASSES // W_CHUNK_PASSES):
            w_words = w_stream.tile([P, W_CHUNK_PASSES, MID], U32, name="w_words", align_bytes=64)
            g0 = chunk * W_CHUNK_PASSES
            nc.sync.dma_start(
                out=w_words[:].bitcast(I32),
                in_=words_by_pass[g0 : g0 + W_CHUNK_PASSES].rearrange("g p n -> p g n"),
            )
            for i in range(TOKEN_TILES):
                for n in range(MID // BANK):
                    n_cols = slice(n * BANK, (n + 1) * BANK)
                    for g_in_chunk in range(W_CHUNK_PASSES):
                        g = g0 + g_in_chunk
                        block, offset = g // PLANES_PER_TILE, 4 * (g % PLANES_PER_TILE)
                        nc.tensor.matmul_mx(
                            out=acc[i][n][:],
                            lhsT=h_codes[:, i, g, :].bitcast(FP8X4),
                            lhsT_scale=h_scales[:, i, g, :],
                            rhs=w_words[:, g_in_chunk, n_cols].bitcast(FP8X4),
                            rhs_scale=w_planes[offset:P, block, n_cols],
                            start=(g == 0),
                            stop=(g == FFN_PASSES - 1),
                        )

        wh_words = keep.tile([P, MID_PASSES, D_OUT], U32, name="wh_words", align_bytes=64)
        nc.sync.dma_start(
            out=wh_words[:].bitcast(I32),
            in_=w_h_words.rearrange("g p n t -> g p (n t)").bitcast(I32).rearrange("g p n -> p g n"),
        )
        for quadrant in range(4):
            nc.sync.dma_start(
                out=wh_planes[32 * quadrant : 32 * quadrant + 4, :, :].bitcast(I32),
                in_=w_h_scales.bitcast(I32)[:, 4 * quadrant : 4 * quadrant + 4, :].rearrange("g q n -> q g n"),
            )

        tail = stack.enter_context(tc.tile_pool(name="tail", bufs=1))

        def per_tile(shape, dtype, name, **options):
            return [
                tail.tile(shape, dtype, name="%s_%d" % (name, i), **options) for i in range(TOKEN_TILES)
            ]

        def half(columns, g):
            return columns[:, g * BANK : (g + 1) * BANK]

        res2 = per_tile([P, MID], F32, "res2")
        row_sums = per_tile([P, MID_PASSES], F32, "row_sums")
        neg_mean = per_tile([P, 1], F32, "neg_mean")
        squares = per_tile([P, MID], BF16, "squares")
        square_sum = per_tile([P, 1], F32, "square_sum")
        rstd = per_tile([P, 1], F32, "rstd")
        gained = per_tile([P, MID], F32, "gained")
        norm2 = per_tile([P, MID], BF16, "norm2")
        norm_grouped = per_tile([P, MID_PASSES, P, PACK], BF16, "norm_grouped", align_bytes=64)
        norm_codes = per_tile([P, MID_PASSES, P], U32, "norm_codes", align_bytes=64)
        norm_scales = per_tile([P, MID_PASSES, P], U8, "norm_scales", align_bytes=64)
        result = per_tile([P, D_OUT], F32, "result")

        def empty_bank(i, g):
            nc.vector.scalar_tensor_tensor(
                out=as_t_j(half(res2[i], g)),
                in0=word_order(acc[i][g][:]),
                scalar=1.0,
                in1=as_t_j(half(residual[i], g)),
                op0=ALU.mult,
                op1=ALU.add,
                accum_out=row_sums[i][:, g : g + 1],
            )

        def statistics(i):
            nc.vector.tensor_scalar(
                out=neg_mean[i][:],
                in0=row_sums[i][:, 0:1],
                scalar1=row_sums[i][:, 1:2],
                scalar2=-1.0 / MID,
                op0=ALU.add,
                op1=ALU.mult,
            )
            nc.scalar.activation(
                out=squares[i][:], in_=res2[i][:], func=ACT.Square, bias=neg_mean[i][:], scale=1.0,
                accum_out=square_sum[i][:],
            )
            nc.scalar.activation(
                out=rstd[i][:], in_=square_sum[i][:], func=ACT.Abs_reciprocal_sqrt, bias=eps[:], scale=1.0 / MID
            )

        def gain(i, g):
            nc.vector.scalar_tensor_tensor(
                out=half(gained[i], g), in0=half(res2[i], g), scalar=neg_mean[i][:],
                in1=half(gain_all, g), op0=ALU.add, op1=ALU.mult,
            )

        with tc.manual_schedule():
            empty_bank(0, 0)
            idle_bank = psum_acc.tile([P, BANK], F32, name="idle_bank", tag="acc_0_0")

            def keep_clock(columns):
                for g in range(MID_PASSES):
                    nc.tensor.matmul(out=idle_bank[:], lhsT=ones[:], rhs=half(columns, g), start=True, stop=True)

            empty_bank(0, 1)
            empty_bank(1, 0)
            statistics(0)
            keep_clock(squares[0])
            empty_bank(1, 1)
            gain(0, 0)
            statistics(1)
            keep_clock(squares[1])
            gain(0, 1)
            gain(1, 0)
            gain(1, 1)

            for i in range(TOKEN_TILES):
                for g in range(MID_PASSES):
                    nc.vector.scalar_tensor_tensor(
                        out=half(norm2[i], g), in0=half(gained[i], g), scalar=rstd[i][:],
                        in1=half(shift_all, g), op0=ALU.mult, op1=ALU.add,
                    )
                    norm_turned = psum_work.tile([P, PACK, P], BF16, name="norm_turned", tag="work")
                    for t in range(PACK):
                        first = (g * PACK + t) * P
                        nc.tensor.transpose(
                            norm_turned[:, t, :], norm2[i][:, first : first + P], ident_bf16[:]
                        )
                    nc.scalar.copy(
                        out=norm_grouped[i][:, g], in_=norm_turned[:].rearrange("p t r -> p r t")
                    )
                    if i == 0 and g == 0:
                        keep_clock(squares[0])

            head = []
            for i in range(TOKEN_TILES):
                head.append(psum_work.tile([P, D_OUT], F32, name="head_%d" % i, tag="work"))
                for g in range(MID_PASSES):
                    nc.vector.quantize_mx(
                        out=norm_codes[i][:, g, :].bitcast(FP8X4),
                        scales=norm_scales[i][:, g, :],
                        in_=norm_grouped[i][:, g].rearrange("p r t -> p (r t)"),
                    )
                    nc.tensor.matmul_mx(
                        out=head[i][:],
                        lhsT=norm_codes[i][:, g, :].bitcast(FP8X4),
                        lhsT_scale=norm_scales[i][:, g, :],
                        rhs=wh_words[:, g, :].bitcast(FP8X4),
                        rhs_scale=wh_planes[:, g, :],
                        start=(g == 0),
                        stop=(g == MID_PASSES - 1),
                    )

            for i in range(TOKEN_TILES):
                nc.vector.tensor_tensor(out=result[i][:], in0=head[i][:], in1=bias_h_all[:], op=ALU.add)
                nc.sync.dma_start(out=out[i], in_=result[i][:])
